import numpy as np
import ml_dtypes


def mxq(x, axis, fmt="e4m3"):
    dtype, down = {"e4m3": (ml_dtypes.float8_e4m3fn, 7), "e5m2": (ml_dtypes.float8_e5m2, 14)}[fmt]
    v = np.moveaxis(np.asarray(x, np.float32).astype(ml_dtypes.bfloat16).astype(np.float64), axis, -1)
    blocks = v.reshape(v.shape[:-1] + (-1, 32))
    amax = np.abs(blocks).max(-1, keepdims=True)
    byte = np.maximum(np.where(amax > 0, np.frexp(amax)[1] - 1 + 127, 0) - down, 1)
    scale = np.exp2(byte - 127.0)
    codes = (blocks / scale).astype(np.float32).astype(dtype).astype(np.float64)
    return np.moveaxis((codes * scale).reshape(v.shape), -1, axis)


WIDE = False


def mx_kscale(k):
    if not WIDE:
        return np.ones(k)
    levels = np.array([10, -10, 5, -5, 0])
    if k % 512:
        return np.exp2(np.random.permutation(np.resize(levels, k // 32))).repeat(32)
    a = np.empty((k // 512, 16))
    for p in range(k // 512):
        a[p, :8] = np.random.permutation(np.resize(levels, 8))
        for g in range(8):
            far = levels[np.abs(levels - a[p, g]) >= 10]
            a[p, g + 8] = far[np.random.randint(len(far))]
    return np.exp2(a.ravel()).repeat(32)


BF16 = ml_dtypes.bfloat16


def bf(x):
    return np.asarray(x, np.float32).astype(BF16)


def f64(x):
    return np.asarray(x).astype(np.float64)


B, IN, HID, PROJ, H, KC = 8192, 128, 512, 512, 4, 4
BH = HID // H
EPS = 1e-5


def silu(v):
    return v / (1.0 + np.exp(-v))


def groupnorm(v, w, b):
    r = v.reshape(B, H, BH)
    mu = r.mean(-1, keepdims=True)
    var = ((r - mu) ** 2).mean(-1, keepdims=True)
    rn = (r - mu) / np.sqrt(var + EPS)
    return rn.reshape(B, HID) * w + b


def draw0():
    s, t = mx_kscale(PROJ), mx_kscale(HID)
    r = np.random.standard_normal
    return {"h_t": bf(r((B, HID)) * 0.5 / np.sqrt(HID)), "x_conv": bf(silu(r((B, PROJ))) * s),
            "x_right": bf(r((B, HID))), "x": bf(r((B, IN))),
            "gn_w": bf((1.0 + 0.1 * r(HID)) * t), "gn_b": bf(0.2 * r(HID) * t),
            "skip_w": bf(r((PROJ, HID)) * 1.5 / np.sqrt(PROJ) / s[:, None] * t[None, :]), "skip_b": bf(0.2 * r(HID) * t),
            "down_w": bf(r((HID, IN)) / np.sqrt(HID) / t[:, None]), "down_b": bf(0.2 * r(IN))}


def core(h_t, x_conv, x_right, x, gn_w, gn_b, skip_w, skip_b, down_w, down_b):
    x_skip = (mxq(f64(x_conv), 1, "e4m3") @ mxq(f64(skip_w), 0, "e4m3")) + f64(skip_b)
    g = (groupnorm(f64(h_t), f64(gn_w), f64(gn_b)) + x_skip) * silu(f64(x_right))
    y = (mxq(g, 1, "e4m3") @ mxq(f64(down_w), 0, "e4m3")) + f64(down_b)
    return y + f64(x)


def e4m3fn_bytes(y):
    return np.clip(np.asarray(y, np.float64), -448.0, 448.0).astype(np.float32).astype(ml_dtypes.float8_e4m3fn).view(np.uint8)


def e4m3fn_values(b):
    return np.asarray(b, np.uint8).view(ml_dtypes.float8_e4m3fn).astype(np.float64)


def setup_inputs():
    d = draw0()
    x0 = np.asarray(d['x_conv']).astype(np.float64)
    s = (np.max(np.abs(x0), axis=(0,), keepdims=True) / 448.0).astype(np.float32)
    out = {}
    for k, v in d.items():
        if k == 'x_conv':
            out['x_conv_bytes'] = e4m3fn_bytes(x0 / s.astype(np.float64))
            out['x_conv_scale'] = s
        else:
            out[k] = v
    return out


def reference(h_t, x_conv_bytes, x_conv_scale, x_right, x, gn_w, gn_b, skip_w, skip_b, down_w, down_b):
    return core(h_t, e4m3fn_values(x_conv_bytes) * x_conv_scale.astype(np.float64), x_right, x, gn_w, gn_b, skip_w, skip_b, down_w, down_b)

@@ -1,0 +1,314 @@
+from contextlib import ExitStack
+
+import concourse.mybir as mybir
+from concourse.masks import make_identity
+
+B, IN, HID, PROJ = 8192, 128, 512, 512
+EPS = 1e-5
+FLOPS = 2 * B * HID * (PROJ + IN)
+
+F32 = mybir.dt.float32
+BF16 = mybir.dt.bfloat16
+U32 = mybir.dt.uint32
+U8 = mybir.dt.uint8
+FP8 = mybir.dt.float8_e4m3fn
+FP8X4 = mybir.dt.float8_e4m3fn_x4
+ACT = mybir.ActivationFunctionType
+ALU = mybir.AluOpType
+
+P = 128
+GROUP = 128
+T = 4
+J = 4
+CH = P * J
+N = B // CH
+GCOLS = 256
+
+
+def tile_mlstmblock_pc_t_kernel(
+    tc, h_t, x_conv_bytes, x_conv_scale, x_right, x, gn_w, gn_b, skip_w, skip_b, down_w, down_b, out
+):
+    nc = tc.nc
+    with ExitStack() as ctx:
+        const = ctx.enter_context(tc.tile_pool(name="const", bufs=1))
+        sb = ctx.enter_context(tc.tile_pool(name="sb", bufs=2))
+        ps = ctx.enter_context(tc.psum_pool(name="ps", bufs=1))
+
+        ident = const.tile([P, P], F32, name="ident")
+        scale = const.tile([P, PROJ], F32, name="scale")
+        w_raw = const.tile([P, T, HID], BF16, name="w_raw")
+        w_grp = const.tile([P, T * P * T], BF16, name="w_grp", align_bytes=64)
+        w_codes = const.tile([P, HID], U32, name="w_codes", align_bytes=64)
+        w_scales = const.tile([P, HID], U8, name="w_scales", align_bytes=64)
+        d_raw = const.tile([P, T, IN], BF16, name="d_raw")
+        d_grp = const.tile([P, IN * T], BF16, name="d_grp", align_bytes=64)
+        d_codes = const.tile([P, IN], U32, name="d_codes", align_bytes=64)
+        d_scales = const.tile([P, IN], U8, name="d_scales", align_bytes=64)
+        gw_raw = const.tile([P, T], BF16, name="gw_raw")
+        gb_raw = const.tile([P, T], BF16, name="gb_raw")
+        sb_raw = const.tile([P, T], BF16, name="sb_raw")
+        gw = const.tile([P, T], F32, name="gw")
+        bias = const.tile([P, T], F32, name="bias")
+        db = const.tile([P, IN], BF16, name="db")
+        neg_half = const.tile([P, J * 4], F32, name="neg_half")
+        warm = const.tile([P, 1], F32, name="warm")
+
+        h_view = h_t.rearrange("(n p j) k -> n p j k", p=P, j=J)
+        xc_view = x_conv_bytes.rearrange("(n p j) k -> n p (j k)", p=P, j=J)
+        xr_view = x_right.rearrange("(n p j) k -> n p j k", p=P, j=J)
+        x_view = x.rearrange("(n p j) d -> n p j d", p=P, j=J)
+        out_view = out.rearrange("(n p j) d -> n p (j d)", p=P, j=J)
+
+        S = [dict() for _ in range(N)]
+
+        def load_h(n):
+            t = sb.tile([P, J, HID], BF16, name="h", tag="h", bufs=4)
+            nc.sync.dma_start(out=t[:], in_=h_view[n])
+            S[n]["h"] = t
+
+        def load_xc(n):
+            t = sb.tile([P, J * PROJ], U8, name="xbytes", tag="xbytes", bufs=3)
+            nc.sync.dma_start(out=t[:], in_=xc_view[n])
+            S[n]["xbytes"] = t
+
+        def load_xr(n):
+            t = sb.tile([P, J, HID], BF16, name="xr", tag="xr", bufs=3)
+            nc.sync.dma_start(out=t[:], in_=xr_view[n])
+            S[n]["xr"] = t
+
+        def load_x(n):
+            t = sb.tile([P, J, IN], BF16, name="xres", tag="xres", bufs=4)
+            nc.sync.dma_start(out=t[:], in_=x_view[n])
+            S[n]["x"] = t
+
+        def v_widen(n):
+            t = sb.tile([P, J * PROJ], BF16, name="xcv", tag="xcv", bufs=2)
+            for j in range(J):
+                c = slice(j * PROJ, (j + 1) * PROJ)
+                nc.vector.tensor_tensor(
+                    out=t[:, c], in0=S[n]["xbytes"][:, c].bitcast(FP8), in1=scale[:], op=ALU.mult
+                )
+            S[n]["xcv"] = t
+
+        def v_stats(n):
+            t = sb.tile([P, J * 2, 6], F32, name="stats", tag="stats", bufs=2)
+            for j in range(J):
+                for a in range(2):
+                    pair = S[n]["h"][:, j, 256 * a : 256 * (a + 1)]
+                    nc.vector.bn_stats(out=t[:, 2 * j + a, :], in_=pair.rearrange("p (e i) -> p i e", e=2))
+            S[n]["stats"] = t
+
+        def v_combine(n, t):
+            if t == 0:
+                S[n]["c"] = sb.tile([P, T, CH], F32, name="c", tag="c", bufs=2)
+            nc.vector.scalar_tensor_tensor(
+                out=S[n]["c"][:, t, :], in0=S[n]["hnT%d" % t][:], scalar=gw[:, t : t + 1],
+                in1=S[n]["xs%d" % t][:], op0=ALU.mult, op1=ALU.add,
+            )
+
+        def gate(eng, n, lo, hi):
+            c = slice(lo, hi)
+            eng.tensor_tensor(
+                out=S[n]["g"][:, c, :].rearrange("p (c i) t -> p c t i", i=4),
+                in0=S[n]["c"][:, :, c].rearrange("p t (c i) -> p c t i", i=4),
+                in1=S[n]["s"][:, :, c].rearrange("p t (c i) -> p c t i", i=4),
+                op=ALU.mult,
+            )
+
+        def new_g(n):
+            S[n]["g"] = sb.tile([P, CH, T], BF16, name="g", tag="g", bufs=2, align_bytes=64)
+
+        def quant(n, src, key):
+            codes = sb.tile([P, CH], U32, name=key + "codes", tag=key + "codes", bufs=2, align_bytes=64)
+            scales = sb.tile([P, CH], U8, name=key + "scales", tag=key + "scales", bufs=2, align_bytes=64)
+            nc.vector.quantize_mx(
+                out=codes[:].bitcast(FP8X4), scales=scales[:], in_=S[n][src][:].rearrange("p n t -> p (n t)")
+            )
+            S[n][key] = (codes, scales)
+
+        def v_out(n):
+            t = sb.tile([P, J * IN], F32, name="yout", tag="yout", bufs=2)
+            nc.vector.tensor_tensor(out=t[:], in0=S[n]["y"][:], in1=S[n]["xb"][:].rearrange("p j d -> p (j d)"), op=ALU.add)
+            nc.sync.dma_start(out=out_view[n], in_=t[:])
+
+        def g_xb(n):
+            t = sb.tile([P, J, IN], F32, name="xb", tag="xb", bufs=2)
+            nc.gpsimd.tensor_tensor(
+                out=t[:], in0=S[n]["x"][:], in1=db[:].unsqueeze(1).to_broadcast([P, J, IN]), op=ALU.add
+            )
+            S[n]["xb"] = t
+
+        def g_stats(n):
+            v = S[n]["stats"][:].rearrange("p a (e c) -> p (a e) c", c=3)
+            var = sb.tile([P, J * 4], F32, name="var", tag="var", bufs=2)
+            rstd = sb.tile([P, J * 4], F32, name="rstd", tag="rstd", bufs=2)
+            nm = sb.tile([P, J * 4], F32, name="nm", tag="nm", bufs=2)
+            nmr = sb.tile([P, J * 4], F32, name="nmr", tag="nmr", bufs=2)
+            nc.gpsimd.tensor_scalar(out=var[:], in0=v[:, :, 2], scalar1=1.0 / GROUP, scalar2=EPS, op0=ALU.mult, op1=ALU.add)
+            nc.gpsimd.tensor_scalar(out=nm[:], in0=v[:, :, 1], scalar1=-1.0, scalar2=0.0, op0=ALU.mult, op1=ALU.add)
+            nc.gpsimd.tensor_tensor(out=rstd[:], in0=var[:], in1=neg_half[:], op=ALU.pow)
+            nc.gpsimd.tensor_tensor(out=nmr[:], in0=nm[:], in1=rstd[:], op=ALU.mult)
+            S[n]["rstd"] = rstd
+            S[n]["nmr"] = nmr
+
+        def s_words(n, b):
+            if b == 0:
+                S[n]["xg"] = sb.tile([P, CH, T], BF16, name="xg", tag="xg", bufs=2, align_bytes=64)
+            words = S[n]["xg"][:].rearrange("p n t -> p (n t)").bitcast(F32).rearrange("p (n u) -> p n u", u=2)
+            nc.scalar.copy(out=words[:, 256 * b : 256 * (b + 1), :], in_=S[n]["xcT%d" % b][:].rearrange("p u n -> p n u"))
+
+        def s_silu(n, b):
+            if b == 0:
+                S[n]["s"] = sb.tile([P, T, CH], F32, name="s", tag="s", bufs=2)
+            src = S[n]["xrT%d" % b][:].rearrange("p u n -> p (u n)").bitcast(BF16)
+            dst = S[n]["s"][:, :, 256 * b : 256 * (b + 1)]
+            nc.scalar.activation(
+                out=dst.rearrange("p (u e) n -> p u e n", e=2),
+                in_=src.rearrange("p (u n e) -> p u e n", u=2, e=2),
+                func=ACT.Silu,
+            )
+
+        def s_norm(n):
+            t = sb.tile([P, J, T, P], F32, name="hn", tag="hn", bufs=2)
+            for j in range(J):
+                for g in range(4):
+                    i = 4 * j + g
+                    nc.scalar.activation(
+                        out=t[:, j, :, 32 * g : 32 * (g + 1)],
+                        in_=S[n]["h"][:, j, GROUP * g : GROUP * (g + 1)].rearrange("p (m t) -> p t m", t=T),
+                        func=ACT.Identity,
+                        scale=S[n]["rstd"][:, i : i + 1],
+                        bias=S[n]["nmr"][:, i : i + 1],
+                    )
+            S[n]["hn"] = t
+
+        def s_skip(n, t):
+            o = sb.tile([P, CH], F32, name="xs", tag="xs", bufs=8)
+            nc.scalar.activation(out=o[:], in_=S[n]["xsT%d" % t][:], func=ACT.Identity, bias=bias[:, t : t + 1])
+            S[n]["xs%d" % t] = o
+
+        def p_words(n, src, key, b):
+            bank = ps.tile([P, 2, 256], F32, name="tr", tag="tr", bufs=2)
+            for jj in range(2):
+                j = 2 * b + jj
+                if src == "xcv":
+                    words = S[n][src][:, j * PROJ : (j + 1) * PROJ].bitcast(F32)
+                else:
+                    words = S[n][src][:, j, :].bitcast(F32)
+                for u in range(2):
+                    nc.tensor.transpose(bank[:, u, P * jj : P * (jj + 1)], words[:, u:256:2], ident[:])
+            S[n]["%s%d" % (key, b)] = bank
+
+        def p_norm(n, t):
+            bank = ps.tile([P, CH], F32, name="hnT", tag="hnT", bufs=3)
+            for j in range(J):
+                nc.tensor.transpose(bank[:, P * j : P * (j + 1)], S[n]["hn"][:, j, t, :], ident[:])
+            S[n]["hnT%d" % t] = bank
+
+        def p_skip(n, t):
+            bank = ps.tile([P, CH], F32, name="xsT", tag="xsT", bufs=2)
+            codes, scales = S[n]["xq"]
+            m = slice(P * t, P * (t + 1))
+            nc.tensor.matmul_mx(
+                out=bank[:], lhsT=w_codes[:, m].bitcast(FP8X4), lhsT_scale=w_scales[:, m],
+                rhs=codes[:].bitcast(FP8X4), rhs_scale=scales[:], start=True, stop=True,
+            )
+            S[n]["xsT%d" % t] = bank
+
+        def p_down(n):
+            bank = ps.tile([P, J * IN], F32, name="y", tag="y", bufs=1)
+            codes, scales = S[n]["gq"]
+            for j in range(J):
+                m = slice(P * j, P * (j + 1))
+                nc.tensor.matmul_mx(
+                    out=bank[:, m], lhsT=codes[:, m].bitcast(FP8X4), lhsT_scale=scales[:, m],
+                    rhs=d_codes[:].bitcast(FP8X4), rhs_scale=d_scales[:], start=True, stop=True,
+                )
+            S[n]["y"] = bank
+
+        def ok(n):
+            return 0 <= n < N
+
+        make_identity(nc, ident[:])
+        nc.gpsimd.memset(neg_half[:], -0.5)
+        nc.vector.memset(warm[:], 0.0)
+
+        with tc.manual_schedule():
+            nc.scalar.activation(out=warm[:], in_=warm[:], func=ACT.Silu)
+            load_h(0)
+            load_xc(0)
+            nc.sync.dma_start(out=scale[:], in_=x_conv_scale.rearrange("o k -> (o k)").partition_broadcast(P))
+            nc.sync.dma_start(out=w_raw[:], in_=skip_w.rearrange("(p j) c -> p j c", j=T))
+            load_h(1)
+            load_xc(1)
+            load_xr(0)
+            nc.sync.dma_start(out=gw_raw[:], in_=gn_w.rearrange("(p t) -> p t", t=T))
+            nc.sync.dma_start(out=gb_raw[:], in_=gn_b.rearrange("(p t) -> p t", t=T))
+            nc.sync.dma_start(out=sb_raw[:], in_=skip_b.rearrange("(p t) -> p t", t=T))
+            nc.sync.dma_start(out=d_raw[:], in_=down_w.rearrange("(p j) d -> p j d", j=T))
+            nc.sync.dma_start(out=db[:], in_=down_b.partition_broadcast(P))
+            load_x(0)
+
+            for n in range(N + 3):
+                if n + 2 < N:
+                    load_h(n + 2)
+                    load_xc(n + 2)
+                if n + 1 < N:
+                    load_xr(n + 1)
+                    load_x(n + 1)
+
+                if ok(n - 2):
+                    v_combine(n - 2, 0)
+                    p_norm(n - 2, 3)
+                    v_combine(n - 2, 1)
+                    v_combine(n - 2, 2)
+                    v_combine(n - 2, 3)
+                    g_xb(n - 2)
+                    new_g(n - 2)
+                    gate(nc.gpsimd, n - 2, CH - GCOLS, CH)
+                if ok(n - 1):
+                    p_words(n - 1, "xcv", "xcT", 0)
+                    s_words(n - 1, 0)
+                    p_words(n - 1, "xcv", "xcT", 1)
+                    s_words(n - 1, 1)
+                if ok(n - 3):
+                    p_down(n - 3)
+                if ok(n - 1):
+                    quant(n - 1, "xg", "xq")
+                if ok(n - 3):
+                    v_out(n - 3)
+                if ok(n):
+                    v_stats(n)
+                    g_stats(n)
+                if n == 0:
+                    nc.scalar.copy(
+                        out=w_grp[:].rearrange("p (t m j) -> p t m j", t=T, j=T),
+                        in_=w_raw[:].rearrange("p j (m t) -> p t m j", t=T),
+                    )
+                    nc.scalar.copy(out=d_grp[:].rearrange("p (d j) -> p d j", j=T), in_=d_raw[:].rearrange("p j d -> p d j"))
+                if ok(n - 2):
+                    gate(nc.vector, n - 2, 0, CH - GCOLS)
+                if ok(n):
+                    v_widen(n)
+                if n == 0:
+                    nc.vector.quantize_mx(out=w_codes[:].bitcast(FP8X4), scales=w_scales[:], in_=w_grp[:])
+                    nc.vector.tensor_tensor(out=bias[:], in0=gb_raw[:], in1=sb_raw[:], op=ALU.add)
+                    nc.vector.tensor_copy(out=gw[:], in_=gw_raw[:])
+                    nc.vector.quantize_mx(out=d_codes[:].bitcast(FP8X4), scales=d_scales[:], in_=d_grp[:])
+                if ok(n - 2):
+                    quant(n - 2, "g", "gq")
+                if ok(n - 1):
+                    p_words(n - 1, "xr", "xrT", 0)
+                    s_silu(n - 1, 0)
+                    p_words(n - 1, "xr", "xrT", 1)
+                    s_silu(n - 1, 1)
+                    p_skip(n - 1, 0)
+                    p_skip(n - 1, 1)
+                    s_norm(n - 1)
+                    for t in range(3):
+                        p_norm(n - 1, t)
+                    s_skip(n - 1, 0)
+                    s_skip(n - 1, 1)
+                    for t in range(2, 4):
+                        p_skip(n - 1, t)
+                        s_skip(n - 1, t)

@@ -11,6 +11,7 @@ F32 = mybir.dt.float32
 BF16 = mybir.dt.bfloat16
 U32 = mybir.dt.uint32
 U8 = mybir.dt.uint8
+I32 = mybir.dt.int32
 FP8 = mybir.dt.float8_e4m3fn
 FP8X4 = mybir.dt.float8_e4m3fn_x4
 ACT = mybir.ActivationFunctionType
@@ -22,7 +23,8 @@ T = 4
 J = 4
 CH = P * J
 N = B // CH
-GCOLS = 256
+SEED = 0x5F3759DF - 0x00400000 - 2**31
+GCOLS = 0
 
 
 def tile_mlstmblock_pc_t_kernel(
@@ -50,7 +52,6 @@ def tile_mlstmblock_pc_t_kernel(
         gw = const.tile([P, T], F32, name="gw")
         bias = const.tile([P, T], F32, name="bias")
         db = const.tile([P, IN], BF16, name="db")
-        neg_half = const.tile([P, J * 4], F32, name="neg_half")
         warm = const.tile([P, 1], F32, name="warm")
 
         h_view = h_t.rearrange("(n p j) k -> n p j k", p=P, j=J)
@@ -62,7 +63,7 @@ def tile_mlstmblock_pc_t_kernel(
         S = [dict() for _ in range(N)]
 
         def load_h(n):
-            t = sb.tile([P, J, HID], BF16, name="h", tag="h", bufs=4)
+            t = sb.tile([P, J, HID], BF16, name="h", tag="h", bufs=6)
             nc.sync.dma_start(out=t[:], in_=h_view[n])
             S[n]["h"] = t
 
@@ -88,15 +89,50 @@ def tile_mlstmblock_pc_t_kernel(
                 nc.vector.tensor_tensor(
                     out=t[:, c], in0=S[n]["xbytes"][:, c].bitcast(FP8), in1=scale[:], op=ALU.mult
                 )
+                tick()
             S[n]["xcv"] = t
 
         def v_stats(n):
-            t = sb.tile([P, J * 2, 6], F32, name="stats", tag="stats", bufs=2)
+            if n % 2 == 0:
+                S[n]["stats"] = sb.tile([P, J * 4, 6], F32, name="stats", tag="stats", bufs=2)
+            t = S[n - n % 2]["stats"]
             for j in range(J):
                 for a in range(2):
                     pair = S[n]["h"][:, j, 256 * a : 256 * (a + 1)]
-                    nc.vector.bn_stats(out=t[:, 2 * j + a, :], in_=pair.rearrange("p (e i) -> p i e", e=2))
-            S[n]["stats"] = t
+                    nc.vector.bn_stats(
+                        out=t[:, 8 * (n % 2) + 2 * j + a, :], in_=pair.rearrange("p (e i) -> p i e", e=2)
+                    )
+            if n % 2 == 1:
+                rstd_steps(n - 1)
+
+        todo = []
+
+        def tick():
+            if todo:
+                todo.pop(0)()
+
+        def rstd_steps(n):
+            W = J * 8
+            v = S[n]["stats"][:].rearrange("p a (e c) -> p (a e) c", c=3)
+            half = sb.tile([P, W], F32, name="half", tag="half", bufs=2)
+            y = sb.tile([P, W], F32, name="rstd", tag="rstd", bufs=2)
+            a = sb.tile([P, W], F32, name="nt_a", tag="nt_a", bufs=2)
+            b = sb.tile([P, W], F32, name="nt_b", tag="nt_b", bufs=2)
+            nmr = sb.tile([P, W], F32, name="nmr", tag="nmr", bufs=2)
+            todo.append(lambda: nc.vector.tensor_scalar(
+                out=half[:], in0=v[:, :, 2], scalar1=0.5 / GROUP, scalar2=0.5 * EPS, op0=ALU.mult, op1=ALU.add))
+            todo.append(lambda: nc.vector.tensor_scalar(
+                out=y[:].bitcast(I32), in0=half[:].bitcast(I32), scalar1=-0.5, scalar2=float(SEED), op0=ALU.mult, op1=ALU.add))
+            for i in range(3):
+                todo.append(lambda: nc.vector.tensor_tensor(out=a[:], in0=y[:], in1=y[:], op=ALU.mult))
+                todo.append(lambda: nc.vector.tensor_tensor(out=b[:], in0=a[:], in1=half[:], op=ALU.mult))
+                todo.append(lambda: nc.vector.scalar_tensor_tensor(
+                    out=y[:], in0=b[:], scalar=1.5, in1=y[:], op0=ALU.subtract, op1=ALU.mult))
+            todo.append(lambda: nc.vector.scalar_tensor_tensor(
+                out=nmr[:], in0=v[:, :, 1], scalar=-1.0, in1=y[:], op0=ALU.mult, op1=ALU.mult))
+            for k in range(2):
+                S[n + k]["rstd"] = y[:, 16 * k : 16 * (k + 1)]
+                S[n + k]["nmr"] = nmr[:, 16 * k : 16 * (k + 1)]
 
         def v_combine(n, t):
             if t == 0:
@@ -105,6 +141,7 @@ def tile_mlstmblock_pc_t_kernel(
                 out=S[n]["c"][:, t, :], in0=S[n]["hnT%d" % t][:], scalar=gw[:, t : t + 1],
                 in1=S[n]["xs%d" % t][:], op0=ALU.mult, op1=ALU.add,
             )
+            tick()
 
         def gate(eng, n, lo, hi):
             c = slice(lo, hi)
@@ -125,10 +162,12 @@ def tile_mlstmblock_pc_t_kernel(
                 out=codes[:].bitcast(FP8X4), scales=scales[:], in_=S[n][src][:].rearrange("p n t -> p (n t)")
             )
             S[n][key] = (codes, scales)
+            tick()
 
         def v_out(n):
             t = sb.tile([P, J * IN], F32, name="yout", tag="yout", bufs=2)
             nc.vector.tensor_tensor(out=t[:], in0=S[n]["y"][:], in1=S[n]["xb"][:].rearrange("p j d -> p (j d)"), op=ALU.add)
+            tick()
             nc.sync.dma_start(out=out_view[n], in_=t[:])
 
         def g_xb(n):
@@ -137,19 +176,6 @@ def tile_mlstmblock_pc_t_kernel(
                 out=t[:], in0=S[n]["x"][:], in1=db[:].unsqueeze(1).to_broadcast([P, J, IN]), op=ALU.add
             )
             S[n]["xb"] = t
-
-        def g_stats(n):
-            v = S[n]["stats"][:].rearrange("p a (e c) -> p (a e) c", c=3)
-            var = sb.tile([P, J * 4], F32, name="var", tag="var", bufs=2)
-            rstd = sb.tile([P, J * 4], F32, name="rstd", tag="rstd", bufs=2)
-            nm = sb.tile([P, J * 4], F32, name="nm", tag="nm", bufs=2)
-            nmr = sb.tile([P, J * 4], F32, name="nmr", tag="nmr", bufs=2)
-            nc.gpsimd.tensor_scalar(out=var[:], in0=v[:, :, 2], scalar1=1.0 / GROUP, scalar2=EPS, op0=ALU.mult, op1=ALU.add)
-            nc.gpsimd.tensor_scalar(out=nm[:], in0=v[:, :, 1], scalar1=-1.0, scalar2=0.0, op0=ALU.mult, op1=ALU.add)
-            nc.gpsimd.tensor_tensor(out=rstd[:], in0=var[:], in1=neg_half[:], op=ALU.pow)
-            nc.gpsimd.tensor_tensor(out=nmr[:], in0=nm[:], in1=rstd[:], op=ALU.mult)
-            S[n]["rstd"] = rstd
-            S[n]["nmr"] = nmr
 
         def s_words(n, b):
             if b == 0:
@@ -230,7 +256,6 @@ def tile_mlstmblock_pc_t_kernel(
             return 0 <= n < N
 
         make_identity(nc, ident[:])
-        nc.gpsimd.memset(neg_half[:], -0.5)
         nc.vector.memset(warm[:], 0.0)
 
         with tc.manual_schedule():
@@ -242,6 +267,7 @@ def tile_mlstmblock_pc_t_kernel(
             load_h(1)
             load_xc(1)
             load_xr(0)
+            load_h(2)
             nc.sync.dma_start(out=gw_raw[:], in_=gn_w.rearrange("(p t) -> p t", t=T))
             nc.sync.dma_start(out=gb_raw[:], in_=gn_b.rearrange("(p t) -> p t", t=T))
             nc.sync.dma_start(out=sb_raw[:], in_=skip_b.rearrange("(p t) -> p t", t=T))
@@ -250,8 +276,9 @@ def tile_mlstmblock_pc_t_kernel(
             load_x(0)
 
             for n in range(N + 3):
-                if n + 2 < N:
-                    load_h(n + 2)
+                if ok(n + 3):
+                    load_h(n + 3)
+                if ok(n + 2):
                     load_xc(n + 2)
                 if n + 1 < N:
                     load_xr(n + 1)
@@ -265,7 +292,8 @@ def tile_mlstmblock_pc_t_kernel(
                     v_combine(n - 2, 3)
                     g_xb(n - 2)
                     new_g(n - 2)
-                    gate(nc.gpsimd, n - 2, CH - GCOLS, CH)
+                    if GCOLS:
+                        gate(nc.gpsimd, n - 2, CH - GCOLS, CH)
                 if ok(n - 1):
                     p_words(n - 1, "xcv", "xcT", 0)
                     s_words(n - 1, 0)
@@ -277,9 +305,12 @@ def tile_mlstmblock_pc_t_kernel(
                     quant(n - 1, "xg", "xq")
                 if ok(n - 3):
                     v_out(n - 3)
-                if ok(n):
-                    v_stats(n)
-                    g_stats(n)
+                while todo:
+                    tick()
+                if n == 0:
+                    v_stats(0)
+                if ok(n + 1):
+                    v_stats(n + 1)
                 if n == 0:
                     nc.scalar.copy(
                         out=w_grp[:].rearrange("p (t m j) -> p t m j", t=T, j=T),
@@ -288,6 +319,7 @@ def tile_mlstmblock_pc_t_kernel(
                     nc.scalar.copy(out=d_grp[:].rearrange("p (d j) -> p d j", j=T), in_=d_raw[:].rearrange("p j d -> p d j"))
                 if ok(n - 2):
                     gate(nc.vector, n - 2, 0, CH - GCOLS)
+                    tick()
                 if ok(n):
                     v_widen(n)
                 if n == 0:

@@ -24,7 +24,7 @@ J = 4
 CH = P * J
 N = B // CH
 SEED = 0x5F3759DF - 0x00400000 - 2**31
-GCOLS = 0
+GCOLS = 192
 
 
 def tile_mlstmblock_pc_t_kernel(
@@ -37,7 +37,8 @@ def tile_mlstmblock_pc_t_kernel(
         ps = ctx.enter_context(tc.psum_pool(name="ps", bufs=1))
 
         ident = const.tile([P, P], F32, name="ident")
-        scale = const.tile([P, PROJ], F32, name="scale")
+        ident_b = const.tile([P, P], BF16, name="ident_b")
+        scale = const.tile([P, J, PROJ], F32, name="scale")
         w_raw = const.tile([P, T, HID], BF16, name="w_raw")
         w_grp = const.tile([P, T * P * T], BF16, name="w_grp", align_bytes=64)
         w_codes = const.tile([P, HID], U32, name="w_codes", align_bytes=64)
@@ -51,7 +52,7 @@ def tile_mlstmblock_pc_t_kernel(
         sb_raw = const.tile([P, T], BF16, name="sb_raw")
         gw = const.tile([P, T], F32, name="gw")
         bias = const.tile([P, T], F32, name="bias")
-        db = const.tile([P, IN], BF16, name="db")
+        db = const.tile([P, 1], BF16, name="db")
         warm = const.tile([P, 1], F32, name="warm")
 
         h_view = h_t.rearrange("(n p j) k -> n p j k", p=P, j=J)
@@ -78,18 +79,16 @@ def tile_mlstmblock_pc_t_kernel(
             S[n]["xr"] = t
 
         def load_x(n):
-            t = sb.tile([P, J, IN], BF16, name="xres", tag="xres", bufs=4)
+            t = sb.tile([P, J, IN], BF16, name="xres", tag="xres", bufs=5)
             nc.sync.dma_start(out=t[:], in_=x_view[n])
             S[n]["x"] = t
 
         def v_widen(n):
             t = sb.tile([P, J * PROJ], BF16, name="xcv", tag="xcv", bufs=2)
-            for j in range(J):
-                c = slice(j * PROJ, (j + 1) * PROJ)
-                nc.vector.tensor_tensor(
-                    out=t[:, c], in0=S[n]["xbytes"][:, c].bitcast(FP8), in1=scale[:], op=ALU.mult
-                )
-                tick()
+            nc.vector.tensor_tensor(
+                out=t[:], in0=S[n]["xbytes"][:].bitcast(FP8), in1=scale[:].rearrange("p j k -> p (j k)"), op=ALU.mult
+            )
+            tick()
             S[n]["xcv"] = t
 
         def v_stats(n):
@@ -102,6 +101,8 @@ def tile_mlstmblock_pc_t_kernel(
                     nc.vector.bn_stats(
                         out=t[:, 8 * (n % 2) + 2 * j + a, :], in_=pair.rearrange("p (e i) -> p i e", e=2)
                     )
+                    if n % 2 == 0:
+                        tick()
             if n % 2 == 1:
                 rstd_steps(n - 1)
 
@@ -143,6 +144,15 @@ def tile_mlstmblock_pc_t_kernel(
             )
             tick()
 
+        def gate_g(n, lo, hi):
+            c = slice(lo, hi)
+            nc.gpsimd.tensor_tensor(
+                out=S[n]["g"][:, c, :],
+                in0=S[n]["c"][:, :, c].rearrange("p t n -> p n t"),
+                in1=S[n]["s"][:, :, c].rearrange("p t n -> p n t"),
+                op=ALU.mult,
+            )
+
         def gate(eng, n, lo, hi):
             c = slice(lo, hi)
             eng.tensor_tensor(
@@ -163,19 +173,6 @@ def tile_mlstmblock_pc_t_kernel(
             )
             S[n][key] = (codes, scales)
             tick()
-
-        def v_out(n):
-            t = sb.tile([P, J * IN], F32, name="yout", tag="yout", bufs=2)
-            nc.vector.tensor_tensor(out=t[:], in0=S[n]["y"][:], in1=S[n]["xb"][:].rearrange("p j d -> p (j d)"), op=ALU.add)
-            tick()
-            nc.sync.dma_start(out=out_view[n], in_=t[:])
-
-        def g_xb(n):
-            t = sb.tile([P, J, IN], F32, name="xb", tag="xb", bufs=2)
-            nc.gpsimd.tensor_tensor(
-                out=t[:], in0=S[n]["x"][:], in1=db[:].unsqueeze(1).to_broadcast([P, J, IN]), op=ALU.add
-            )
-            S[n]["xb"] = t
 
         def s_words(n, b):
             if b == 0:
@@ -213,6 +210,16 @@ def tile_mlstmblock_pc_t_kernel(
             nc.scalar.activation(out=o[:], in_=S[n]["xsT%d" % t][:], func=ACT.Identity, bias=bias[:, t : t + 1])
             S[n]["xs%d" % t] = o
 
+        def s_down(n):
+            t = sb.tile([P, CH], F32, name="yT", tag="yT", bufs=2)
+            nc.scalar.activation(out=t[:], in_=S[n]["y"][:], func=ACT.Identity, bias=db[:, 0:1])
+            S[n]["yT"] = t
+
+        def s_out(n):
+            t = sb.tile([P, J * IN], F32, name="yout", tag="yout", bufs=2)
+            nc.scalar.copy(out=t[:], in_=S[n]["o"][:])
+            nc.sync.dma_start(out=out_view[n], in_=t[:])
+
         def p_words(n, src, key, b):
             bank = ps.tile([P, 2, 256], F32, name="tr", tag="tr", bufs=2)
             for jj in range(2):
@@ -242,27 +249,38 @@ def tile_mlstmblock_pc_t_kernel(
             S[n]["xsT%d" % t] = bank
 
         def p_down(n):
-            bank = ps.tile([P, J * IN], F32, name="y", tag="y", bufs=1)
+            bank = ps.tile([P, CH], F32, name="y", tag="y", bufs=1)
             codes, scales = S[n]["gq"]
+            nc.tensor.matmul_mx(
+                out=bank[:], lhsT=d_codes[:].bitcast(FP8X4), lhsT_scale=d_scales[:],
+                rhs=codes[:].bitcast(FP8X4), rhs_scale=scales[:], start=True, stop=True,
+            )
+            S[n]["y"] = bank
+
+        def p_out(n):
+            bank = ps.tile([P, CH], F32, name="y", tag="y", bufs=1)
+            nc.tensor.matmul(
+                bank[:], lhsT=ident_b[:], rhs=S[n]["x"][:].rearrange("p j d -> p (j d)"), start=True, stop=False
+            )
             for j in range(J):
                 m = slice(P * j, P * (j + 1))
-                nc.tensor.matmul_mx(
-                    out=bank[:, m], lhsT=codes[:, m].bitcast(FP8X4), lhsT_scale=scales[:, m],
-                    rhs=d_codes[:].bitcast(FP8X4), rhs_scale=d_scales[:], start=True, stop=True,
+                nc.tensor.matmul(
+                    bank[:, m], lhsT=S[n]["yT"][:, m], rhs=ident[:], start=False, stop=(j == J - 1), is_transpose=True
                 )
-            S[n]["y"] = bank
+            S[n]["o"] = bank
 
         def ok(n):
             return 0 <= n < N
 
         make_identity(nc, ident[:])
+        make_identity(nc, ident_b[:])
         nc.vector.memset(warm[:], 0.0)
 
         with tc.manual_schedule():
             nc.scalar.activation(out=warm[:], in_=warm[:], func=ACT.Silu)
             load_h(0)
             load_xc(0)
-            nc.sync.dma_start(out=scale[:], in_=x_conv_scale.rearrange("o k -> (o k)").partition_broadcast(P))
+            nc.sync.dma_start(out=scale[:, 0, :], in_=x_conv_scale.rearrange("o k -> (o k)").partition_broadcast(P))
             nc.sync.dma_start(out=w_raw[:], in_=skip_w.rearrange("(p j) c -> p j c", j=T))
             load_h(1)
             load_xc(1)
@@ -272,8 +290,10 @@ def tile_mlstmblock_pc_t_kernel(
             nc.sync.dma_start(out=gb_raw[:], in_=gn_b.rearrange("(p t) -> p t", t=T))
             nc.sync.dma_start(out=sb_raw[:], in_=skip_b.rearrange("(p t) -> p t", t=T))
             nc.sync.dma_start(out=d_raw[:], in_=down_w.rearrange("(p j) d -> p j d", j=T))
-            nc.sync.dma_start(out=db[:], in_=down_b.partition_broadcast(P))
+            nc.sync.dma_start(out=db[:], in_=down_b.rearrange("(d o) -> d o", o=1))
             load_x(0)
+            for j in range(1, J):
+                nc.scalar.copy(out=scale[:, j, :], in_=scale[:, 0, :])
 
             for n in range(N + 3):
                 if ok(n + 3):
@@ -287,13 +307,11 @@ def tile_mlstmblock_pc_t_kernel(
                 if ok(n - 2):
                     v_combine(n - 2, 0)
                     p_norm(n - 2, 3)
-                    v_combine(n - 2, 1)
-                    v_combine(n - 2, 2)
-                    v_combine(n - 2, 3)
-                    g_xb(n - 2)
+                    for t in range(1, T):
+                        v_combine(n - 2, t)
                     new_g(n - 2)
                     if GCOLS:
-                        gate(nc.gpsimd, n - 2, CH - GCOLS, CH)
+                        gate_g(n - 2, CH - GCOLS, CH)
                 if ok(n - 1):
                     p_words(n - 1, "xcv", "xcT", 0)
                     s_words(n - 1, 0)
@@ -301,22 +319,22 @@ def tile_mlstmblock_pc_t_kernel(
                     s_words(n - 1, 1)
                 if ok(n - 3):
                     p_down(n - 3)
-                if ok(n - 1):
-                    quant(n - 1, "xg", "xq")
-                if ok(n - 3):
-                    v_out(n - 3)
-                while todo:
-                    tick()
+                    s_down(n - 3)
                 if n == 0:
                     v_stats(0)
                 if ok(n + 1):
                     v_stats(n + 1)
+                if n % 2 == 1:
+                    while todo:
+                        tick()
                 if n == 0:
                     nc.scalar.copy(
                         out=w_grp[:].rearrange("p (t m j) -> p t m j", t=T, j=T),
                         in_=w_raw[:].rearrange("p j (m t) -> p t m j", t=T),
                     )
                     nc.scalar.copy(out=d_grp[:].rearrange("p (d j) -> p d j", j=T), in_=d_raw[:].rearrange("p j d -> p d j"))
+                if ok(n - 1):
+                    quant(n - 1, "xg", "xq")
                 if ok(n - 2):
                     gate(nc.vector, n - 2, 0, CH - GCOLS)
                     tick()
@@ -334,6 +352,10 @@ def tile_mlstmblock_pc_t_kernel(
                     s_silu(n - 1, 0)
                     p_words(n - 1, "xr", "xrT", 1)
                     s_silu(n - 1, 1)
+                if ok(n - 3):
+                    p_out(n - 3)
+                    s_out(n - 3)
+                if ok(n - 1):
                     p_skip(n - 1, 0)
                     p_skip(n - 1, 1)
                     s_norm(n - 1)
@@ -341,6 +363,6 @@ def tile_mlstmblock_pc_t_kernel(
                         p_norm(n - 1, t)
                     s_skip(n - 1, 0)
                     s_skip(n - 1, 1)
-                    for t in range(2, 4):
+                    for t in range(2, T):
                         p_skip(n - 1, t)
                         s_skip(n - 1, t)

@@ -24,7 +24,7 @@ J = 4
 CH = P * J
 N = B // CH
 SEED = 0x5F3759DF - 0x00400000 - 2**31
-GCOLS = 192
+GCOLS = 0
 
 
 def tile_mlstmblock_pc_t_kernel(
@@ -69,17 +69,17 @@ def tile_mlstmblock_pc_t_kernel(
             S[n]["h"] = t
 
         def load_xc(n):
-            t = sb.tile([P, J * PROJ], U8, name="xbytes", tag="xbytes", bufs=3)
+            t = sb.tile([P, J * PROJ], U8, name="xbytes", tag="xbytes", bufs=4)
             nc.sync.dma_start(out=t[:], in_=xc_view[n])
             S[n]["xbytes"] = t
 
         def load_xr(n):
-            t = sb.tile([P, J, HID], BF16, name="xr", tag="xr", bufs=3)
+            t = sb.tile([P, J, HID], BF16, name="xr", tag="xr", bufs=4)
             nc.sync.dma_start(out=t[:], in_=xr_view[n])
             S[n]["xr"] = t
 
         def load_x(n):
-            t = sb.tile([P, J, IN], BF16, name="xres", tag="xres", bufs=5)
+            t = sb.tile([P, J, IN], BF16, name="xres", tag="xres", bufs=4)
             nc.sync.dma_start(out=t[:], in_=x_view[n])
             S[n]["x"] = t
 
@@ -166,8 +166,8 @@ def tile_mlstmblock_pc_t_kernel(
             S[n]["g"] = sb.tile([P, CH, T], BF16, name="g", tag="g", bufs=2, align_bytes=64)
 
         def quant(n, src, key):
-            codes = sb.tile([P, CH], U32, name=key + "codes", tag=key + "codes", bufs=2, align_bytes=64)
-            scales = sb.tile([P, CH], U8, name=key + "scales", tag=key + "scales", bufs=2, align_bytes=64)
+            codes = sb.tile([P, CH], U32, name=key + "codes", tag=key + "codes", bufs=3, align_bytes=64)
+            scales = sb.tile([P, CH], U8, name=key + "scales", tag=key + "scales", bufs=3, align_bytes=64)
             nc.vector.quantize_mx(
                 out=codes[:].bitcast(FP8X4), scales=scales[:], in_=S[n][src][:].rearrange("p n t -> p (n t)")
             )
@@ -182,7 +182,7 @@ def tile_mlstmblock_pc_t_kernel(
 
         def s_silu(n, b):
             if b == 0:
-                S[n]["s"] = sb.tile([P, T, CH], F32, name="s", tag="s", bufs=2)
+                S[n]["s"] = sb.tile([P, T, CH], F32, name="s", tag="s", bufs=3)
             src = S[n]["xrT%d" % b][:].rearrange("p u n -> p (u n)").bitcast(BF16)
             dst = S[n]["s"][:, :, 256 * b : 256 * (b + 1)]
             nc.scalar.activation(
@@ -192,18 +192,17 @@ def tile_mlstmblock_pc_t_kernel(
             )
 
         def s_norm(n):
-            t = sb.tile([P, J, T, P], F32, name="hn", tag="hn", bufs=2)
+            S[n]["hn"] = sb.tile([P, J, T, P], F32, name="hn", tag="hn", bufs=2)
             for j in range(J):
                 for g in range(4):
                     i = 4 * j + g
                     nc.scalar.activation(
-                        out=t[:, j, :, 32 * g : 32 * (g + 1)],
+                        out=S[n]["hn"][:, j, :, 32 * g : 32 * (g + 1)],
                         in_=S[n]["h"][:, j, GROUP * g : GROUP * (g + 1)].rearrange("p (m t) -> p t m", t=T),
                         func=ACT.Identity,
                         scale=S[n]["rstd"][:, i : i + 1],
                         bias=S[n]["nmr"][:, i : i + 1],
                     )
-            S[n]["hn"] = t
 
         def s_skip(n, t):
             o = sb.tile([P, CH], F32, name="xs", tag="xs", bufs=8)
@@ -233,7 +232,7 @@ def tile_mlstmblock_pc_t_kernel(
             S[n]["%s%d" % (key, b)] = bank
 
         def p_norm(n, t):
-            bank = ps.tile([P, CH], F32, name="hnT", tag="hnT", bufs=3)
+            bank = ps.tile([P, CH], F32, name="hnT", tag="hnT", bufs=4)
             for j in range(J):
                 nc.tensor.transpose(bank[:, P * j : P * (j + 1)], S[n]["hn"][:, j, t, :], ident[:])
             S[n]["hnT%d" % t] = bank
@@ -249,7 +248,7 @@ def tile_mlstmblock_pc_t_kernel(
             S[n]["xsT%d" % t] = bank
 
         def p_down(n):
-            bank = ps.tile([P, CH], F32, name="y", tag="y", bufs=1)
+            bank = ps.tile([P, CH], F32, name="tr", tag="tr", bufs=2)
             codes, scales = S[n]["gq"]
             nc.tensor.matmul_mx(
                 out=bank[:], lhsT=d_codes[:].bitcast(FP8X4), lhsT_scale=d_scales[:],
@@ -258,7 +257,7 @@ def tile_mlstmblock_pc_t_kernel(
             S[n]["y"] = bank
 
         def p_out(n):
-            bank = ps.tile([P, CH], F32, name="y", tag="y", bufs=1)
+            bank = ps.tile([P, CH], F32, name="tr", tag="tr", bufs=2)
             nc.tensor.matmul(
                 bank[:], lhsT=ident_b[:], rhs=S[n]["x"][:].rearrange("p j d -> p (j d)"), start=True, stop=False
             )
@@ -291,35 +290,54 @@ def tile_mlstmblock_pc_t_kernel(
             nc.sync.dma_start(out=sb_raw[:], in_=skip_b.rearrange("(p t) -> p t", t=T))
             nc.sync.dma_start(out=d_raw[:], in_=down_w.rearrange("(p j) d -> p j d", j=T))
             nc.sync.dma_start(out=db[:], in_=down_b.rearrange("(d o) -> d o", o=1))
-            load_x(0)
             for j in range(1, J):
                 nc.scalar.copy(out=scale[:, j, :], in_=scale[:, 0, :])
 
-            for n in range(N + 3):
+            for n in range(N + 4):
                 if ok(n + 3):
                     load_h(n + 3)
                 if ok(n + 2):
                     load_xc(n + 2)
-                if n + 1 < N:
+                if ok(n + 1):
                     load_xr(n + 1)
-                    load_x(n + 1)
-
                 if ok(n - 2):
-                    v_combine(n - 2, 0)
-                    p_norm(n - 2, 3)
-                    for t in range(1, T):
-                        v_combine(n - 2, t)
-                    new_g(n - 2)
-                    if GCOLS:
-                        gate_g(n - 2, CH - GCOLS, CH)
+                    load_x(n - 2)
+                if ok(n - 2):
+                    p_skip(n - 2, 0)
+                    s_skip(n - 2, 0)
+                    p_skip(n - 2, 1)
+                    s_skip(n - 2, 1)
+                if ok(n - 4):
+                    p_down(n - 4)
+                    s_down(n - 4)
                 if ok(n - 1):
-                    p_words(n - 1, "xcv", "xcT", 0)
-                    s_words(n - 1, 0)
-                    p_words(n - 1, "xcv", "xcT", 1)
-                    s_words(n - 1, 1)
+                    for b in range(2):
+                        p_words(n - 1, "xcv", "xcT", b)
+                        s_words(n - 1, b)
+                if ok(n - 4):
+                    p_out(n - 4)
+                    s_out(n - 4)
+                if ok(n - 1):
+                    p_words(n - 1, "xr", "xrT", 0)
+                    s_silu(n - 1, 0)
+                if ok(n - 2):
+                    p_skip(n - 2, 2)
+                    s_skip(n - 2, 2)
+                    p_skip(n - 2, 3)
+                    s_skip(n - 2, 3)
+                if ok(n - 1):
+                    p_words(n - 1, "xr", "xrT", 1)
+                    s_silu(n - 1, 1)
+
                 if ok(n - 3):
-                    p_down(n - 3)
-                    s_down(n - 3)
+                    for t in range(T):
+                        v_combine(n - 3, t)
+                    new_g(n - 3)
+                    if GCOLS:
+                        gate_g(n - 3, CH - GCOLS, CH)
+                if ok(n - 2):
+                    for t in range(T):
+                        p_norm(n - 2, t)
                 if n == 0:
                     v_stats(0)
                 if ok(n + 1):
@@ -327,16 +345,16 @@ def tile_mlstmblock_pc_t_kernel(
                 if n % 2 == 1:
                     while todo:
                         tick()
+                if ok(n - 1):
+                    s_norm(n - 1)
                 if n == 0:
                     nc.scalar.copy(
                         out=w_grp[:].rearrange("p (t m j) -> p t m j", t=T, j=T),
                         in_=w_raw[:].rearrange("p j (m t) -> p t m j", t=T),
                     )
                     nc.scalar.copy(out=d_grp[:].rearrange("p (d j) -> p d j", j=T), in_=d_raw[:].rearrange("p j d -> p d j"))
-                if ok(n - 1):
-                    quant(n - 1, "xg", "xq")
-                if ok(n - 2):
-                    gate(nc.vector, n - 2, 0, CH - GCOLS)
+                if ok(n - 3):
+                    gate(nc.vector, n - 3, 0, CH - GCOLS)
                     tick()
                 if ok(n):
                     v_widen(n)
@@ -345,24 +363,7 @@ def tile_mlstmblock_pc_t_kernel(
                     nc.vector.tensor_tensor(out=bias[:], in0=gb_raw[:], in1=sb_raw[:], op=ALU.add)
                     nc.vector.tensor_copy(out=gw[:], in_=gw_raw[:])
                     nc.vector.quantize_mx(out=d_codes[:].bitcast(FP8X4), scales=d_scales[:], in_=d_grp[:])
-                if ok(n - 2):
-                    quant(n - 2, "g", "gq")
                 if ok(n - 1):
-                    p_words(n - 1, "xr", "xrT", 0)
-                    s_silu(n - 1, 0)
-                    p_words(n - 1, "xr", "xrT", 1)
-                    s_silu(n - 1, 1)
+                    quant(n - 1, "xg", "xq")
                 if ok(n - 3):
-                    p_out(n - 3)
-                    s_out(n - 3)
-                if ok(n - 1):
-                    p_skip(n - 1, 0)
-                    p_skip(n - 1, 1)
-                    s_norm(n - 1)
-                    for t in range(3):
-                        p_norm(n - 1, t)
-                    s_skip(n - 1, 0)
-                    s_skip(n - 1, 1)
-                    for t in range(2, T):
-                        p_skip(n - 1, t)
-                        s_skip(n - 1, t)
+                    quant(n - 3, "g", "gq")

from contextlib import ExitStack

import concourse.mybir as mybir
from concourse.masks import make_identity

B, IN, HID, PROJ = 8192, 128, 512, 512
EPS = 1e-5
FLOPS = 2 * B * HID * (PROJ + IN)

F32 = mybir.dt.float32
BF16 = mybir.dt.bfloat16
U32 = mybir.dt.uint32
U8 = mybir.dt.uint8
I32 = mybir.dt.int32
FP8 = mybir.dt.float8_e4m3fn
FP8X4 = mybir.dt.float8_e4m3fn_x4
ACT = mybir.ActivationFunctionType
ALU = mybir.AluOpType

P = 128
GROUP = 128
T = 4
J = 4
CH = P * J
N = B // CH
SEED = 0x5F3759DF - 0x00400000 - 2**31
GCOLS = 0


def tile_mlstmblock_pc_t_kernel(
    tc, h_t, x_conv_bytes, x_conv_scale, x_right, x, gn_w, gn_b, skip_w, skip_b, down_w, down_b, out
):
    nc = tc.nc
    with ExitStack() as ctx:
        const = ctx.enter_context(tc.tile_pool(name="const", bufs=1))
        sb = ctx.enter_context(tc.tile_pool(name="sb", bufs=2))
        ps = ctx.enter_context(tc.psum_pool(name="ps", bufs=1))

        ident = const.tile([P, P], F32, name="ident")
        ident_b = const.tile([P, P], BF16, name="ident_b")
        scale = const.tile([P, J, PROJ], F32, name="scale")
        w_raw = const.tile([P, T, HID], BF16, name="w_raw")
        w_grp = const.tile([P, T * P * T], BF16, name="w_grp", align_bytes=64)
        w_codes = const.tile([P, HID], U32, name="w_codes", align_bytes=64)
        w_scales = const.tile([P, HID], U8, name="w_scales", align_bytes=64)
        d_raw = const.tile([P, T, IN], BF16, name="d_raw")
        d_grp = const.tile([P, IN * T], BF16, name="d_grp", align_bytes=64)
        d_codes = const.tile([P, IN], U32, name="d_codes", align_bytes=64)
        d_scales = const.tile([P, IN], U8, name="d_scales", align_bytes=64)
        gw_raw = const.tile([P, T], BF16, name="gw_raw")
        gb_raw = const.tile([P, T], BF16, name="gb_raw")
        sb_raw = const.tile([P, T], BF16, name="sb_raw")
        gw = const.tile([P, T], F32, name="gw")
        bias = const.tile([P, T], F32, name="bias")
        db = const.tile([P, 1], BF16, name="db")
        warm = const.tile([P, 1], F32, name="warm")

        h_view = h_t.rearrange("(n p j) k -> n p j k", p=P, j=J)
        xc_view = x_conv_bytes.rearrange("(n p j) k -> n p (j k)", p=P, j=J)
        xr_view = x_right.rearrange("(n p j) k -> n p j k", p=P, j=J)
        x_view = x.rearrange("(n p j) d -> n p j d", p=P, j=J)
        out_view = out.rearrange("(n p j) d -> n p (j d)", p=P, j=J)

        S = [dict() for _ in range(N)]

        def load_h(n):
            t = sb.tile([P, J, HID], BF16, name="h", tag="h", bufs=6)
            nc.sync.dma_start(out=t[:], in_=h_view[n])
            S[n]["h"] = t

        def load_xc(n):
            t = sb.tile([P, J * PROJ], U8, name="xbytes", tag="xbytes", bufs=4)
            nc.sync.dma_start(out=t[:], in_=xc_view[n])
            S[n]["xbytes"] = t

        def load_xr(n):
            t = sb.tile([P, J, HID], BF16, name="xr", tag="xr", bufs=4)
            nc.sync.dma_start(out=t[:], in_=xr_view[n])
            S[n]["xr"] = t

        def load_x(n):
            t = sb.tile([P, J, IN], BF16, name="xres", tag="xres", bufs=4)
            nc.sync.dma_start(out=t[:], in_=x_view[n])
            S[n]["x"] = t

        def v_widen(n):
            t = sb.tile([P, J * PROJ], BF16, name="xcv", tag="xcv", bufs=2)
            nc.vector.tensor_tensor(
                out=t[:], in0=S[n]["xbytes"][:].bitcast(FP8), in1=scale[:].rearrange("p j k -> p (j k)"), op=ALU.mult
            )
            tick()
            S[n]["xcv"] = t

        def v_stats(n):
            if n % 2 == 0:
                S[n]["stats"] = sb.tile([P, J * 4, 6], F32, name="stats", tag="stats", bufs=2)
            t = S[n - n % 2]["stats"]
            for j in range(J):
                for a in range(2):
                    pair = S[n]["h"][:, j, 256 * a : 256 * (a + 1)]
                    nc.vector.bn_stats(
                        out=t[:, 8 * (n % 2) + 2 * j + a, :], in_=pair.rearrange("p (e i) -> p i e", e=2)
                    )
                    if n % 2 == 0:
                        tick()
            if n % 2 == 1:
                rstd_steps(n - 1)

        todo = []

        def tick():
            if todo:
                todo.pop(0)()

        def rstd_steps(n):
            W = J * 8
            v = S[n]["stats"][:].rearrange("p a (e c) -> p (a e) c", c=3)
            half = sb.tile([P, W], F32, name="half", tag="half", bufs=2)
            y = sb.tile([P, W], F32, name="rstd", tag="rstd", bufs=2)
            a = sb.tile([P, W], F32, name="nt_a", tag="nt_a", bufs=2)
            b = sb.tile([P, W], F32, name="nt_b", tag="nt_b", bufs=2)
            nmr = sb.tile([P, W], F32, name="nmr", tag="nmr", bufs=2)
            todo.append(lambda: nc.vector.tensor_scalar(
                out=half[:], in0=v[:, :, 2], scalar1=0.5 / GROUP, scalar2=0.5 * EPS, op0=ALU.mult, op1=ALU.add))
            todo.append(lambda: nc.vector.tensor_scalar(
                out=y[:].bitcast(I32), in0=half[:].bitcast(I32), scalar1=-0.5, scalar2=float(SEED), op0=ALU.mult, op1=ALU.add))
            for i in range(3):
                todo.append(lambda: nc.vector.tensor_tensor(out=a[:], in0=y[:], in1=y[:], op=ALU.mult))
                todo.append(lambda: nc.vector.tensor_tensor(out=b[:], in0=a[:], in1=half[:], op=ALU.mult))
                todo.append(lambda: nc.vector.scalar_tensor_tensor(
                    out=y[:], in0=b[:], scalar=1.5, in1=y[:], op0=ALU.subtract, op1=ALU.mult))
            todo.append(lambda: nc.vector.scalar_tensor_tensor(
                out=nmr[:], in0=v[:, :, 1], scalar=-1.0, in1=y[:], op0=ALU.mult, op1=ALU.mult))
            for k in range(2):
                S[n + k]["rstd"] = y[:, 16 * k : 16 * (k + 1)]
                S[n + k]["nmr"] = nmr[:, 16 * k : 16 * (k + 1)]

        def v_combine(n, t):
            if t == 0:
                S[n]["c"] = sb.tile([P, T, CH], F32, name="c", tag="c", bufs=2)
            nc.vector.scalar_tensor_tensor(
                out=S[n]["c"][:, t, :], in0=S[n]["hnT%d" % t][:], scalar=gw[:, t : t + 1],
                in1=S[n]["xs%d" % t][:], op0=ALU.mult, op1=ALU.add,
            )
            tick()

        def gate_g(n, lo, hi):
            c = slice(lo, hi)
            nc.gpsimd.tensor_tensor(
                out=S[n]["g"][:, c, :],
                in0=S[n]["c"][:, :, c].rearrange("p t n -> p n t"),
                in1=S[n]["s"][:, :, c].rearrange("p t n -> p n t"),
                op=ALU.mult,
            )

        def gate(eng, n, lo, hi):
            c = slice(lo, hi)
            eng.tensor_tensor(
                out=S[n]["g"][:, c, :].rearrange("p (c i) t -> p c t i", i=4),
                in0=S[n]["c"][:, :, c].rearrange("p t (c i) -> p c t i", i=4),
                in1=S[n]["s"][:, :, c].rearrange("p t (c i) -> p c t i", i=4),
                op=ALU.mult,
            )

        def new_g(n):
            S[n]["g"] = sb.tile([P, CH, T], BF16, name="g", tag="g", bufs=2, align_bytes=64)

        def quant(n, src, key):
            codes = sb.tile([P, CH], U32, name=key + "codes", tag=key + "codes", bufs=3, align_bytes=64)
            scales = sb.tile([P, CH], U8, name=key + "scales", tag=key + "scales", bufs=3, align_bytes=64)
            nc.vector.quantize_mx(
                out=codes[:].bitcast(FP8X4), scales=scales[:], in_=S[n][src][:].rearrange("p n t -> p (n t)")
            )
            S[n][key] = (codes, scales)
            tick()

        def s_words(n, b):
            if b == 0:
                S[n]["xg"] = sb.tile([P, CH, T], BF16, name="xg", tag="xg", bufs=2, align_bytes=64)
            words = S[n]["xg"][:].rearrange("p n t -> p (n t)").bitcast(F32).rearrange("p (n u) -> p n u", u=2)
            nc.scalar.copy(out=words[:, 256 * b : 256 * (b + 1), :], in_=S[n]["xcT%d" % b][:].rearrange("p u n -> p n u"))

        def s_silu(n, b):
            if b == 0:
                S[n]["s"] = sb.tile([P, T, CH], F32, name="s", tag="s", bufs=3)
            src = S[n]["xrT%d" % b][:].rearrange("p u n -> p (u n)").bitcast(BF16)
            dst = S[n]["s"][:, :, 256 * b : 256 * (b + 1)]
            nc.scalar.activation(
                out=dst.rearrange("p (u e) n -> p u e n", e=2),
                in_=src.rearrange("p (u n e) -> p u e n", u=2, e=2),
                func=ACT.Silu,
            )

        def s_norm(n):
            S[n]["hn"] = sb.tile([P, J, T, P], F32, name="hn", tag="hn", bufs=2)
            for j in range(J):
                for g in range(4):
                    i = 4 * j + g
                    nc.scalar.activation(
                        out=S[n]["hn"][:, j, :, 32 * g : 32 * (g + 1)],
                        in_=S[n]["h"][:, j, GROUP * g : GROUP * (g + 1)].rearrange("p (m t) -> p t m", t=T),
                        func=ACT.Identity,
                        scale=S[n]["rstd"][:, i : i + 1],
                        bias=S[n]["nmr"][:, i : i + 1],
                    )

        def s_skip(n, t):
            o = sb.tile([P, CH], F32, name="xs", tag="xs", bufs=8)
            nc.scalar.activation(out=o[:], in_=S[n]["xsT%d" % t][:], func=ACT.Identity, bias=bias[:, t : t + 1])
            S[n]["xs%d" % t] = o

        def s_down(n):
            t = sb.tile([P, CH], F32, name="yT", tag="yT", bufs=2)
            nc.scalar.activation(out=t[:], in_=S[n]["y"][:], func=ACT.Identity, bias=db[:, 0:1])
            S[n]["yT"] = t

        def s_out(n):
            t = sb.tile([P, J * IN], F32, name="yout", tag="yout", bufs=2)
            nc.scalar.copy(out=t[:], in_=S[n]["o"][:])
            nc.sync.dma_start(out=out_view[n], in_=t[:])

        def p_words(n, src, key, b):
            bank = ps.tile([P, 2, 256], F32, name="tr", tag="tr", bufs=2)
            for jj in range(2):
                j = 2 * b + jj
                if src == "xcv":
                    words = S[n][src][:, j * PROJ : (j + 1) * PROJ].bitcast(F32)
                else:
                    words = S[n][src][:, j, :].bitcast(F32)
                for u in range(2):
                    nc.tensor.transpose(bank[:, u, P * jj : P * (jj + 1)], words[:, u:256:2], ident[:])
            S[n]["%s%d" % (key, b)] = bank

        def p_norm(n, t):
            bank = ps.tile([P, CH], F32, name="hnT", tag="hnT", bufs=4)
            for j in range(J):
                nc.tensor.transpose(bank[:, P * j : P * (j + 1)], S[n]["hn"][:, j, t, :], ident[:])
            S[n]["hnT%d" % t] = bank

        def p_skip(n, t):
            bank = ps.tile([P, CH], F32, name="xsT", tag="xsT", bufs=2)
            codes, scales = S[n]["xq"]
            m = slice(P * t, P * (t + 1))
            nc.tensor.matmul_mx(
                out=bank[:], lhsT=w_codes[:, m].bitcast(FP8X4), lhsT_scale=w_scales[:, m],
                rhs=codes[:].bitcast(FP8X4), rhs_scale=scales[:], start=True, stop=True,
            )
            S[n]["xsT%d" % t] = bank

        def p_down(n):
            bank = ps.tile([P, CH], F32, name="tr", tag="tr", bufs=2)
            codes, scales = S[n]["gq"]
            nc.tensor.matmul_mx(
                out=bank[:], lhsT=d_codes[:].bitcast(FP8X4), lhsT_scale=d_scales[:],
                rhs=codes[:].bitcast(FP8X4), rhs_scale=scales[:], start=True, stop=True,
            )
            S[n]["y"] = bank

        def p_out(n):
            bank = ps.tile([P, CH], F32, name="tr", tag="tr", bufs=2)
            nc.tensor.matmul(
                bank[:], lhsT=ident_b[:], rhs=S[n]["x"][:].rearrange("p j d -> p (j d)"), start=True, stop=False
            )
            for j in range(J):
                m = slice(P * j, P * (j + 1))
                nc.tensor.matmul(
                    bank[:, m], lhsT=S[n]["yT"][:, m], rhs=ident[:], start=False, stop=(j == J - 1), is_transpose=True
                )
            S[n]["o"] = bank

        def ok(n):
            return 0 <= n < N

        make_identity(nc, ident[:])
        make_identity(nc, ident_b[:])
        nc.vector.memset(warm[:], 0.0)

        with tc.manual_schedule():
            nc.scalar.activation(out=warm[:], in_=warm[:], func=ACT.Silu)
            load_h(0)
            load_xc(0)
            nc.sync.dma_start(out=scale[:, 0, :], in_=x_conv_scale.rearrange("o k -> (o k)").partition_broadcast(P))
            nc.sync.dma_start(out=w_raw[:], in_=skip_w.rearrange("(p j) c -> p j c", j=T))
            load_h(1)
            load_xc(1)
            load_xr(0)
            load_h(2)
            nc.sync.dma_start(out=gw_raw[:], in_=gn_w.rearrange("(p t) -> p t", t=T))
            nc.sync.dma_start(out=gb_raw[:], in_=gn_b.rearrange("(p t) -> p t", t=T))
            nc.sync.dma_start(out=sb_raw[:], in_=skip_b.rearrange("(p t) -> p t", t=T))
            nc.sync.dma_start(out=d_raw[:], in_=down_w.rearrange("(p j) d -> p j d", j=T))
            nc.sync.dma_start(out=db[:], in_=down_b.rearrange("(d o) -> d o", o=1))
            for j in range(1, J):
                nc.scalar.copy(out=scale[:, j, :], in_=scale[:, 0, :])

            for n in range(N + 4):
                if ok(n + 3):
                    load_h(n + 3)
                if ok(n + 2):
                    load_xc(n + 2)
                if ok(n + 1):
                    load_xr(n + 1)
                if ok(n - 2):
                    load_x(n - 2)
                if ok(n - 2):
                    p_skip(n - 2, 0)
                    s_skip(n - 2, 0)
                    p_skip(n - 2, 1)
                    s_skip(n - 2, 1)
                if ok(n - 4):
                    p_down(n - 4)
                    s_down(n - 4)
                if ok(n - 1):
                    for b in range(2):
                        p_words(n - 1, "xcv", "xcT", b)
                        s_words(n - 1, b)
                if ok(n - 4):
                    p_out(n - 4)
                    s_out(n - 4)
                if ok(n - 1):
                    p_words(n - 1, "xr", "xrT", 0)
                    s_silu(n - 1, 0)
                if ok(n - 2):
                    p_skip(n - 2, 2)
                    s_skip(n - 2, 2)
                    p_skip(n - 2, 3)
                    s_skip(n - 2, 3)
                if ok(n - 1):
                    p_words(n - 1, "xr", "xrT", 1)
                    s_silu(n - 1, 1)

                if ok(n - 3):
                    for t in range(T):
                        v_combine(n - 3, t)
                    new_g(n - 3)
                    if GCOLS:
                        gate_g(n - 3, CH - GCOLS, CH)
                if ok(n - 2):
                    for t in range(T):
                        p_norm(n - 2, t)
                if n == 0:
                    v_stats(0)
                if ok(n + 1):
                    v_stats(n + 1)
                if n % 2 == 1:
                    while todo:
                        tick()
                if ok(n - 1):
                    s_norm(n - 1)
                if n == 0:
                    nc.scalar.copy(
                        out=w_grp[:].rearrange("p (t m j) -> p t m j", t=T, j=T),
                        in_=w_raw[:].rearrange("p j (m t) -> p t m j", t=T),
                    )
                    nc.scalar.copy(out=d_grp[:].rearrange("p (d j) -> p d j", j=T), in_=d_raw[:].rearrange("p j d -> p d j"))
                if ok(n - 3):
                    gate(nc.vector, n - 3, 0, CH - GCOLS)
                    tick()
                if ok(n):
                    v_widen(n)
                if n == 0:
                    nc.vector.quantize_mx(out=w_codes[:].bitcast(FP8X4), scales=w_scales[:], in_=w_grp[:])
                    nc.vector.tensor_tensor(out=bias[:], in0=gb_raw[:], in1=sb_raw[:], op=ALU.add)
                    nc.vector.tensor_copy(out=gw[:], in_=gw_raw[:])
                    nc.vector.quantize_mx(out=d_codes[:].bitcast(FP8X4), scales=d_scales[:], in_=d_grp[:])
                if ok(n - 1):
                    quant(n - 1, "xg", "xq")
                if ok(n - 3):
                    quant(n - 3, "g", "gq")
